import numpy as np
import ml_dtypes


def mxq(x, axis, fmt="e4m3"):
    dtype, down = {"e4m3": (ml_dtypes.float8_e4m3fn, 7), "e5m2": (ml_dtypes.float8_e5m2, 14)}[fmt]
    v = np.moveaxis(np.asarray(x, np.float32).astype(ml_dtypes.bfloat16).astype(np.float64), axis, -1)
    blocks = v.reshape(v.shape[:-1] + (-1, 32))
    amax = np.abs(blocks).max(-1, keepdims=True)
    byte = np.maximum(np.where(amax > 0, np.frexp(amax)[1] - 1 + 127, 0) - down, 1)
    scale = np.exp2(byte - 127.0)
    codes = (blocks / scale).astype(np.float32).astype(dtype).astype(np.float64)
    return np.moveaxis((codes * scale).reshape(v.shape), -1, axis)


WIDE = False


def mx_kscale(k):
    if not WIDE:
        return np.ones(k)
    levels = np.array([10, -10, 5, -5, 0])
    a = np.random.permutation(np.resize(levels, k // 512 * 4)).reshape(k // 512, 4)
    idx = np.arange(k)
    return np.exp2(a[idx // 512, idx % 128 // 32])


BF16 = ml_dtypes.bfloat16


def bf(x):
    return np.asarray(x, np.float32).astype(BF16)


def f64(x):
    return np.asarray(x).astype(np.float64)


B, CIN, H, W, CP, G = 8, 1024, 32, 32, 128, 8
CG = CP // G
HW = H * W
ATT_N = np.sqrt(HW * HW * CG / CIN + HW * CG)


def setup_inputs():
    s = mx_kscale(CIN)
    r = np.sqrt(2.5 / ATT_N) / np.sqrt(CIN)
    return {"x": bf(np.random.standard_normal((B, CIN, H, W)) * s[None, :, None, None]),
            "Wt": bf(np.random.standard_normal((CP, CIN)) / np.sqrt(CIN) / s),
            "Wp": bf(np.random.standard_normal((CP, CIN)) * r / s),
            "Wg": bf(np.random.standard_normal((CP, CIN)) * r / s)}


def reference(x, Wt, Wp, Wg):
    xq = mxq(f64(x).reshape(B, CIN, HW), 1, "e4m3")
    t = mxq(f64(Wt), 1, "e4m3") @ xq
    p = mxq(f64(Wp), 1, "e4m3") @ xq
    g = mxq(f64(Wg), 1, "e4m3") @ xq
    t = t.reshape(B, G, CG * HW)
    p = p.reshape(B, G, CG * HW)
    g = g.reshape(B, G, CG * HW)
    att = (p * g).sum(-1, keepdims=True)
    return (att * t).reshape(B, G, CG, HW)

@@ -1,0 +1,259 @@
+from contextlib import ExitStack
+
+import concourse.mybir as mybir
+from concourse.masks import make_identity
+
+F32 = mybir.dt.float32
+BF16 = mybir.dt.bfloat16
+U32 = mybir.dt.uint32
+U8 = mybir.dt.uint8
+FP8X4 = mybir.dt.float8_e4m3fn_x4
+ALU = mybir.AluOpType
+ACT = mybir.ActivationFunctionType
+AX = mybir.AxisListType
+
+IMAGES = 8
+K = 1024
+HW = 1024
+P = 128
+PACK = 4
+K_PASS = P * PACK
+PASSES = K // K_PASS
+N_TILE = 512
+HALVES = HW // N_TILE
+CHUNKS = IMAGES * PASSES
+GROUP = 16
+
+FLOPS = 2 * IMAGES * 3 * P * K * HW
+
+PIN = True
+V_COLS = 592
+
+
+def tile_spatialcgnl_pa_t_kernel(tc, x, Wt, Wp, Wg, out):
+    nc = tc.nc
+    xv = x.rearrange("b k h w -> b k (h w)")
+    ov = out.rearrange("b g c n -> b (g c) n")
+
+    with ExitStack() as ctx:
+        const = ctx.enter_context(tc.tile_pool(name="const", bufs=1))
+        rawp = ctx.enter_context(tc.tile_pool(name="rawp", bufs=CHUNKS))
+        grpp = ctx.enter_context(tc.tile_pool(name="grpp", bufs=3))
+        codp = ctx.enter_context(tc.tile_pool(name="codp", bufs=4))
+        wrk = ctx.enter_context(tc.tile_pool(name="wrk", bufs=3))
+        psum = ctx.enter_context(tc.psum_pool(name="psum", bufs=2))
+        if PIN:
+            ctx.enter_context(tc.manual_schedule())
+
+        raw = {}
+        grouped = {}
+        codes = {}
+        scales = {}
+        w_raw = {}
+        w_ps = {}
+        w_grp = {}
+        w_codes = {}
+        w_scales = {}
+        p_ps = {}
+        g_ps = {}
+        t_ps = {}
+        p_sb = {}
+        acc = {}
+        att_sb = {}
+        o_sb = {}
+
+        def pieces(n):
+            if n == 0:
+                return [(0, 512), (512, 1024)]
+            return [(0, HW)]
+
+        def split(w0, w1):
+            v = (w1 - w0) * V_COLS // HW
+            v = v - v % 8
+            return w0 + v
+
+        def load(n):
+            b, c = divmod(n, PASSES)
+            raw[n] = rawp.tile([P, PACK, HW], BF16, name="raw", tag="raw")
+            src = xv[b, c * K_PASS : (c + 1) * K_PASS, :].rearrange("(p j) n -> p j n", j=PACK)
+            for w0, w1 in pieces(n):
+                nc.sync.dma_start(out=raw[n][:, :, w0:w1], in_=src[:, :, w0:w1])
+
+        def regroup_views(n, w0, w1):
+            dst = grouped[n][:, w0:w1, :].rearrange("p (c i) t -> p c t i", i=4)
+            src = raw[n][:, :, w0:w1].rearrange("p t (c i) -> p c t i", i=4)
+            return dst, src
+
+        def new_grouped(n):
+            grouped[n] = grpp.tile([P, HW, PACK], BF16, name="grouped", tag="grouped", align_bytes=64)
+
+        def rg_v(n):
+            for w0, w1 in pieces(n):
+                dst, src = regroup_views(n, w0, split(w0, w1))
+                nc.vector.tensor_copy(out=dst, in_=src)
+
+        def rg_s(n):
+            for w0, w1 in pieces(n):
+                dst, src = regroup_views(n, split(w0, w1), w1)
+                nc.scalar.copy(out=dst, in_=src)
+
+        def quant(n):
+            codes[n] = codp.tile([P, HW], U32, name="codes", tag="codes", align_bytes=64)
+            scales[n] = codp.tile([P, HW], U8, name="scales", tag="scales", align_bytes=64)
+            nc.vector.quantize_mx(
+                out=codes[n][:].bitcast(FP8X4),
+                scales=scales[n][:],
+                in_=grouped[n][:].rearrange("p w j -> p (w j)"),
+            )
+
+        def mx(acc_ps, w, b, c, h, start, stop):
+            n = b * PASSES + c
+            m_cols = slice(c * P, (c + 1) * P)
+            n_cols = slice(h * N_TILE, (h + 1) * N_TILE)
+            nc.tensor.matmul_mx(
+                out=acc_ps[:],
+                lhsT=w_codes[w][:, m_cols].bitcast(FP8X4),
+                lhsT_scale=w_scales[w][:, m_cols],
+                rhs=codes[n][:, n_cols].bitcast(FP8X4),
+                rhs_scale=scales[n][:, n_cols],
+                start=start,
+                stop=stop,
+            )
+
+        def mm_pg_c0(b):
+            for h in range(HALVES):
+                p_ps[b, h] = psum.tile([P, N_TILE], F32, name="p_ps", tag="p")
+                mx(p_ps[b, h], "p", b, 0, h, True, False)
+                g_ps[b, h] = psum.tile([P, N_TILE], F32, name="g_ps", tag="g")
+                mx(g_ps[b, h], "g", b, 0, h, True, False)
+
+        def mm_pg_c1(b):
+            for h in range(HALVES):
+                mx(p_ps[b, h], "p", b, 1, h, False, True)
+                mx(g_ps[b, h], "g", b, 1, h, False, True)
+
+        def mm_t(b):
+            for h in range(HALVES):
+                t_ps[b, h] = psum.tile([P, N_TILE], F32, name="t_ps", tag="t")
+                mx(t_ps[b, h], "t", b, 0, h, True, False)
+                mx(t_ps[b, h], "t", b, 1, h, False, True)
+
+        def p_copy(b, h):
+            p_sb[b, h] = wrk.tile([P, N_TILE], F32, name="p_sb", tag="p_sb")
+            nc.scalar.copy(out=p_sb[b, h][:], in_=p_ps[b, h][:])
+
+        def pg_sum(b, h):
+            if h == 0:
+                acc[b] = wrk.tile([P, HALVES], F32, name="acc", tag="acc")
+            junk = wrk.tile([P, N_TILE], F32, name="junk", tag="junk", bufs=2)
+            nc.vector.scalar_tensor_tensor(
+                out=junk[:],
+                in0=g_ps[b, h][:],
+                scalar=1.0,
+                in1=p_sb[b, h][:],
+                op0=ALU.mult,
+                op1=ALU.mult,
+                accum_out=acc[b][:, h : h + 1],
+            )
+
+        def att_mm(b):
+            att_ps = psum.tile([P, HALVES], F32, name="att_ps", tag="att", bufs=1)
+            nc.tensor.matmul(att_ps[:], lhsT=blk2d, rhs=acc[b][:], start=True, stop=True)
+            return att_ps
+
+        def att_copy(b, att_ps):
+            att_sb[b] = wrk.tile([P, 1], F32, name="att_sb", tag="att_sb")
+            att_junk = wrk.tile([P, HALVES], F32, name="att_junk", tag="att_junk")
+            nc.scalar.activation(out=att_junk[:], in_=att_ps[:], func=ACT.Copy, accum_out=att_sb[b][:])
+
+        def t_out(b, h, on_vector):
+            if h == 0:
+                o_sb[b] = wrk.tile([P, HW], F32, name="o_sb", tag="o_sb")
+            dst = o_sb[b][:, h * N_TILE : (h + 1) * N_TILE]
+            if on_vector:
+                nc.vector.tensor_scalar_mul(out=dst, in0=t_ps[b, h][:], scalar1=att_sb[b][:, 0:1])
+            else:
+                nc.scalar.activation(out=dst, in_=t_ps[b, h][:], func=ACT.Copy, scale=att_sb[b][:, 0:1])
+
+        def store(b):
+            nc.sync.dma_start(out=ov[b], in_=o_sb[b][:])
+
+        load(0)
+        for w, ap in (("p", Wp), ("g", Wg), ("t", Wt)):
+            w_raw[w] = const.tile([P, K], BF16, name="w_raw_" + w)
+            nc.sync.dma_start(out=w_raw[w][:], in_=ap)
+        for n in range(1, CHUNKS):
+            load(n)
+
+        warm_in = const.tile([P, 1], F32, name="warm_in")
+        warm_out = const.tile([P, 1], F32, name="warm_out")
+        nc.vector.memset(warm_in[:], 0.0)
+        nc.scalar.activation(out=warm_out[:], in_=warm_in[:], func=ACT.Copy)
+        ident = const.tile([P, P], F32, name="ident")
+        make_identity(nc, ident[:])
+
+        new_grouped(0)
+        rg_v(0)
+        rg_s(0)
+        for w in ("p", "g", "t"):
+            w_ps[w] = psum.tile([P, PASSES * 2, P], F32, name="w_ps", tag=w)
+            words = w_raw[w][:].bitcast(F32).rearrange("m (c p u) -> m c u p", c=PASSES, u=2)
+            for c in range(PASSES):
+                for u in range(2):
+                    nc.tensor.transpose(w_ps[w][:, c * 2 + u, :], words[:, c, u, :], ident[:])
+        quant(0)
+        for w in ("p", "g", "t"):
+            w_grp[w] = const.tile([P, PASSES * P * PACK], BF16, name="w_grp_" + w, align_bytes=64)
+            dst = w_grp[w][:].bitcast(F32).rearrange("p (c m u) -> p c m u", c=PASSES, u=2)
+            src = w_ps[w][:].rearrange("p (c u) m -> p c m u", c=PASSES)
+            if w == "t":
+                nc.vector.tensor_copy(out=dst, in_=src)
+            else:
+                nc.scalar.copy(out=dst, in_=src)
+        for w in ("p", "g", "t"):
+            w_codes[w] = const.tile([P, PASSES * P], U32, name="w_codes_" + w, align_bytes=64)
+            w_scales[w] = const.tile([P, PASSES * P], U8, name="w_scales_" + w, align_bytes=64)
+            nc.vector.quantize_mx(
+                out=w_codes[w][:].bitcast(FP8X4), scales=w_scales[w][:], in_=w_grp[w][:]
+            )
+        mm_pg_c0(0)
+        new_grouped(1)
+        rg_v(1)
+        rg_s(1)
+        grp8 = const.tile([P, P // GROUP], F32, name="grp8")
+        nc.vector.reduce_sum(out=grp8[:], in_=ident[:].rearrange("p (j i) -> p j i", i=GROUP), axis=AX.X)
+        blk = const.tile([P, P // GROUP, GROUP], F32, name="blk")
+        nc.vector.tensor_copy(out=blk[:], in_=grp8[:].unsqueeze(2).to_broadcast([P, P // GROUP, GROUP]))
+        blk2d = blk[:].rearrange("p j i -> p (j i)")
+        new_grouped(2)
+        rg_v(2)
+        rg_s(2)
+        quant(1)
+
+        for b in range(IMAGES):
+            last = b == IMAGES - 1
+            mm_pg_c1(b)
+            p_copy(b, 0)
+            p_copy(b, 1)
+            mm_t(b)
+            if not last:
+                new_grouped(2 * b + 3)
+                rg_v(2 * b + 3)
+            pg_sum(b, 0)
+            pg_sum(b, 1)
+            if not last:
+                rg_s(2 * b + 3)
+            att_ps = att_mm(b)
+            if not last:
+                quant(2 * b + 2)
+                mm_pg_c0(b + 1)
+            att_copy(b, att_ps)
+            t_out(b, 0, False)
+            t_out(b, 1, last)
+            store(b)
+            if 2 * b + 4 < CHUNKS:
+                new_grouped(2 * b + 4)
+                rg_v(2 * b + 4)
+                rg_s(2 * b + 4)
+            if not last:
+                quant(2 * b + 3)

@@ -27,7 +27,7 @@ GROUP = 16
 FLOPS = 2 * IMAGES * 3 * P * K * HW
 
 PIN = True
-V_COLS = 592
+V_COLS = [592, 592, 592, 464, 496, 600, 600, 600, 600, 600, 600, 600, 600, 704, 576, 592]
 
 
 def tile_spatialcgnl_pa_t_kernel(tc, x, Wt, Wp, Wg, out):
@@ -67,8 +67,8 @@ def tile_spatialcgnl_pa_t_kernel(tc, x, Wt, Wp, Wg, out):
                 return [(0, 512), (512, 1024)]
             return [(0, HW)]
 
-        def split(w0, w1):
-            v = (w1 - w0) * V_COLS // HW
+        def split(n, w0, w1):
+            v = (w1 - w0) * V_COLS[n] // HW
             v = v - v % 8
             return w0 + v
 
@@ -89,26 +89,27 @@ def tile_spatialcgnl_pa_t_kernel(tc, x, Wt, Wp, Wg, out):
 
         def rg_v(n):
             for w0, w1 in pieces(n):
-                dst, src = regroup_views(n, w0, split(w0, w1))
+                dst, src = regroup_views(n, w0, split(n, w0, w1))
                 nc.vector.tensor_copy(out=dst, in_=src)
 
         def rg_s(n):
             for w0, w1 in pieces(n):
-                dst, src = regroup_views(n, split(w0, w1), w1)
+                dst, src = regroup_views(n, split(n, w0, w1), w1)
                 nc.scalar.copy(out=dst, in_=src)
 
-        def quant(n):
-            codes[n] = codp.tile([P, HW], U32, name="codes", tag="codes", align_bytes=64)
-            scales[n] = codp.tile([P, HW], U8, name="scales", tag="scales", align_bytes=64)
+        def quant(n, w0=0, w1=HW):
+            if w0 == 0:
+                codes[n] = codp.tile([P, HW], U32, name="codes", tag="codes", align_bytes=64)
+                scales[n] = codp.tile([P, HW], U8, name="scales", tag="scales", align_bytes=64)
             nc.vector.quantize_mx(
-                out=codes[n][:].bitcast(FP8X4),
-                scales=scales[n][:],
-                in_=grouped[n][:].rearrange("p w j -> p (w j)"),
+                out=codes[n][:, w0:w1].bitcast(FP8X4),
+                scales=scales[n][:, w0:w1],
+                in_=grouped[n][:, w0:w1, :].rearrange("p w j -> p (w j)"),
             )
 
         def mx(acc_ps, w, b, c, h, start, stop):
             n = b * PASSES + c
-            m_cols = slice(c * P, (c + 1) * P)
+            m_cols = slice(w_base[w] + c * P, w_base[w] + (c + 1) * P)
             n_cols = slice(h * N_TILE, (h + 1) * N_TILE)
             nc.tensor.matmul_mx(
                 out=acc_ps[:],
@@ -120,23 +121,34 @@ def tile_spatialcgnl_pa_t_kernel(tc, x, Wt, Wp, Wg, out):
                 stop=stop,
             )
 
+        def p_c0(b, h):
+            p_ps[b, h] = psum.tile([P, N_TILE], F32, name="p_ps", tag="p")
+            mx(p_ps[b, h], "p", b, 0, h, True, False)
+
+        def g_c0(b, h):
+            g_ps[b, h] = psum.tile([P, N_TILE], F32, name="g_ps", tag="g")
+            mx(g_ps[b, h], "g", b, 0, h, True, False)
+
+        def p_c1(b, h):
+            mx(p_ps[b, h], "p", b, 1, h, False, True)
+
+        def g_c1(b, h):
+            mx(g_ps[b, h], "g", b, 1, h, False, True)
+
         def mm_pg_c0(b):
             for h in range(HALVES):
-                p_ps[b, h] = psum.tile([P, N_TILE], F32, name="p_ps", tag="p")
-                mx(p_ps[b, h], "p", b, 0, h, True, False)
-                g_ps[b, h] = psum.tile([P, N_TILE], F32, name="g_ps", tag="g")
-                mx(g_ps[b, h], "g", b, 0, h, True, False)
+                p_c0(b, h)
+                g_c0(b, h)
 
         def mm_pg_c1(b):
             for h in range(HALVES):
-                mx(p_ps[b, h], "p", b, 1, h, False, True)
-                mx(g_ps[b, h], "g", b, 1, h, False, True)
+                p_c1(b, h)
+                g_c1(b, h)
 
-        def mm_t(b):
-            for h in range(HALVES):
-                t_ps[b, h] = psum.tile([P, N_TILE], F32, name="t_ps", tag="t")
-                mx(t_ps[b, h], "t", b, 0, h, True, False)
-                mx(t_ps[b, h], "t", b, 1, h, False, True)
+        def mm_t(b, h):
+            t_ps[b, h] = psum.tile([P, N_TILE], F32, name="t_ps", tag="t", bufs=3)
+            mx(t_ps[b, h], "t", b, 0, h, True, False)
+            mx(t_ps[b, h], "t", b, 1, h, False, True)
 
         def p_copy(b, h):
             p_sb[b, h] = wrk.tile([P, N_TILE], F32, name="p_sb", tag="p_sb")
@@ -178,11 +190,34 @@ def tile_spatialcgnl_pa_t_kernel(tc, x, Wt, Wp, Wg, out):
         def store(b):
             nc.sync.dma_start(out=ov[b], in_=o_sb[b][:])
 
-        load(0)
-        for w, ap in (("p", Wp), ("g", Wg), ("t", Wt)):
+        def load_w(w, ap):
             w_raw[w] = const.tile([P, K], BF16, name="w_raw_" + w)
             nc.sync.dma_start(out=w_raw[w][:], in_=ap)
-        for n in range(1, CHUNKS):
+
+        def w_transpose(w):
+            w_ps[w] = psum.tile([P, PASSES * 2, P], F32, name="w_ps", tag=w, bufs=3 if w == "t" else 2)
+            words = w_raw[w][:].bitcast(F32).rearrange("m (c p u) -> m c u p", c=PASSES, u=2)
+            for c in range(PASSES):
+                for u in range(2):
+                    nc.tensor.transpose(w_ps[w][:, c * 2 + u, :], words[:, c, u, :], ident[:])
+
+        def w_copy(w):
+            cols = slice(w_base[w] * PACK, (w_base[w] + PASSES * P) * PACK)
+            dst = w_grp[w][:, cols].bitcast(F32).rearrange("p (c m u) -> p c m u", c=PASSES, u=2)
+            src = w_ps[w][:].rearrange("p (c u) m -> p c m u", c=PASSES)
+            nc.scalar.copy(out=dst, in_=src)
+
+        def w_quant(w):
+            nc.vector.quantize_mx(
+                out=w_codes[w][:].bitcast(FP8X4), scales=w_scales[w][:], in_=w_grp[w][:]
+            )
+
+        load(0)
+        load_w("p", Wp)
+        load_w("g", Wg)
+        load(1)
+        load_w("t", Wt)
+        for n in range(2, CHUNKS):
             load(n)
 
         warm_in = const.tile([P, 1], F32, name="warm_in")
@@ -192,68 +227,102 @@ def tile_spatialcgnl_pa_t_kernel(tc, x, Wt, Wp, Wg, out):
         ident = const.tile([P, P], F32, name="ident")
         make_identity(nc, ident[:])
 
+        w_base = {"p": 0, "g": PASSES * P, "t": 0}
+        pg_grp = const.tile([P, 2 * PASSES * P * PACK], BF16, name="pg_grp", align_bytes=64)
+        pg_codes = const.tile([P, 2 * PASSES * P], U32, name="pg_codes", align_bytes=64)
+        pg_scales = const.tile([P, 2 * PASSES * P], U8, name="pg_scales", align_bytes=64)
+        t_grp = const.tile([P, PASSES * P * PACK], BF16, name="t_grp", align_bytes=64)
+        t_codes = const.tile([P, PASSES * P], U32, name="t_codes", align_bytes=64)
+        t_scales = const.tile([P, PASSES * P], U8, name="t_scales", align_bytes=64)
+        for w in ("p", "g"):
+            w_grp[w] = pg_grp
+            w_codes[w] = pg_codes
+            w_scales[w] = pg_scales
+        w_grp["t"] = t_grp
+        w_codes["t"] = t_codes
+        w_scales["t"] = t_scales
+
         new_grouped(0)
         rg_v(0)
         rg_s(0)
-        for w in ("p", "g", "t"):
-            w_ps[w] = psum.tile([P, PASSES * 2, P], F32, name="w_ps", tag=w)
-            words = w_raw[w][:].bitcast(F32).rearrange("m (c p u) -> m c u p", c=PASSES, u=2)
-            for c in range(PASSES):
-                for u in range(2):
-                    nc.tensor.transpose(w_ps[w][:, c * 2 + u, :], words[:, c, u, :], ident[:])
+        w_transpose("p")
+        w_transpose("g")
+        w_copy("p")
+        w_copy("g")
         quant(0)
-        for w in ("p", "g", "t"):
-            w_grp[w] = const.tile([P, PASSES * P * PACK], BF16, name="w_grp_" + w, align_bytes=64)
-            dst = w_grp[w][:].bitcast(F32).rearrange("p (c m u) -> p c m u", c=PASSES, u=2)
-            src = w_ps[w][:].rearrange("p (c u) m -> p c m u", c=PASSES)
-            if w == "t":
-                nc.vector.tensor_copy(out=dst, in_=src)
-            else:
-                nc.scalar.copy(out=dst, in_=src)
-        for w in ("p", "g", "t"):
-            w_codes[w] = const.tile([P, PASSES * P], U32, name="w_codes_" + w, align_bytes=64)
-            w_scales[w] = const.tile([P, PASSES * P], U8, name="w_scales_" + w, align_bytes=64)
-            nc.vector.quantize_mx(
-                out=w_codes[w][:].bitcast(FP8X4), scales=w_scales[w][:], in_=w_grp[w][:]
-            )
+        w_quant("p")
         mm_pg_c0(0)
         new_grouped(1)
         rg_v(1)
         rg_s(1)
+        w_transpose("t")
+        w_copy("t")
         grp8 = const.tile([P, P // GROUP], F32, name="grp8")
         nc.vector.reduce_sum(out=grp8[:], in_=ident[:].rearrange("p (j i) -> p j i", i=GROUP), axis=AX.X)
         blk = const.tile([P, P // GROUP, GROUP], F32, name="blk")
         nc.vector.tensor_copy(out=blk[:], in_=grp8[:].unsqueeze(2).to_broadcast([P, P // GROUP, GROUP]))
         blk2d = blk[:].rearrange("p j i -> p (j i)")
+        quant(1)
+        w_quant("t")
         new_grouped(2)
         rg_v(2)
         rg_s(2)
-        quant(1)
 
-        for b in range(IMAGES):
-            last = b == IMAGES - 1
+        for b in range(IMAGES - 2):
             mm_pg_c1(b)
+            mm_t(b, 0)
+            mm_t(b, 1)
             p_copy(b, 0)
             p_copy(b, 1)
-            mm_t(b)
-            if not last:
-                new_grouped(2 * b + 3)
-                rg_v(2 * b + 3)
+            new_grouped(2 * b + 3)
+            rg_v(2 * b + 3)
+            quant(2 * b + 2)
             pg_sum(b, 0)
             pg_sum(b, 1)
-            if not last:
-                rg_s(2 * b + 3)
+            mm_pg_c0(b + 1)
             att_ps = att_mm(b)
-            if not last:
-                quant(2 * b + 2)
-                mm_pg_c0(b + 1)
+            rg_s(2 * b + 3)
+            new_grouped(2 * b + 4)
+            rg_v(2 * b + 4)
+            rg_s(2 * b + 4)
             att_copy(b, att_ps)
             t_out(b, 0, False)
-            t_out(b, 1, last)
+            t_out(b, 1, False)
             store(b)
-            if 2 * b + 4 < CHUNKS:
-                new_grouped(2 * b + 4)
-                rg_v(2 * b + 4)
-                rg_s(2 * b + 4)
-            if not last:
-                quant(2 * b + 3)
+            quant(2 * b + 3)
+
+        mm_pg_c1(6)
+        mm_t(6, 0)
+        mm_t(6, 1)
+        new_grouped(15)
+        rg_v(15)
+        rg_s(15)
+        p_copy(6, 0)
+        p_copy(6, 1)
+        quant(14)
+        quant(15, 0, N_TILE)
+        quant(15, N_TILE, HW)
+        pg_sum(6, 0)
+        pg_sum(6, 1)
+        for h in range(HALVES):
+            p_c0(7, h)
+            p_c1(7, h)
+        for h in range(HALVES):
+            g_c0(7, h)
+            g_c1(7, h)
+        att_ps = att_mm(6)
+        mm_t(7, 0)
+        p_copy(7, 0)
+        p_copy(7, 1)
+        att_copy(6, att_ps)
+        t_out(6, 0, False)
+        t_out(6, 1, False)
+        store(6)
+        pg_sum(7, 0)
+        pg_sum(7, 1)
+        att_ps = att_mm(7)
+        mm_t(7, 1)
+        att_copy(7, att_ps)
+        t_out(7, 0, False)
+        t_out(7, 1, True)
+        store(7)

@@ -27,7 +27,7 @@ GROUP = 16
 FLOPS = 2 * IMAGES * 3 * P * K * HW
 
 PIN = True
-V_COLS = [592, 592, 592, 464, 496, 600, 600, 600, 600, 600, 600, 600, 600, 704, 576, 592]
+V_COLS = [632, 632, 632, 504, 536, 640, 640, 640, 640, 640, 640, 640, 640, 744, 616, 632]
 
 
 def tile_spatialcgnl_pa_t_kernel(tc, x, Wt, Wp, Wg, out):

@@ -27,7 +27,7 @@ GROUP = 16
 FLOPS = 2 * IMAGES * 3 * P * K * HW
 
 PIN = True
-V_COLS = [632, 632, 632, 504, 536, 640, 640, 640, 640, 640, 640, 640, 640, 744, 616, 632]
+V_COLS = [592, 592, 592, 464, 496, 600, 600, 600, 600, 600, 600, 600, 600, 704, 576, 592]
 
 
 def tile_spatialcgnl_pa_t_kernel(tc, x, Wt, Wp, Wg, out):
@@ -63,8 +63,6 @@ def tile_spatialcgnl_pa_t_kernel(tc, x, Wt, Wp, Wg, out):
         o_sb = {}
 
         def pieces(n):
-            if n == 0:
-                return [(0, 512), (512, 1024)]
             return [(0, HW)]
 
         def split(n, w0, w1):
@@ -271,7 +269,6 @@ def tile_spatialcgnl_pa_t_kernel(tc, x, Wt, Wp, Wg, out):
         for b in range(IMAGES - 2):
             mm_pg_c1(b)
             mm_t(b, 0)
-            mm_t(b, 1)
             p_copy(b, 0)
             p_copy(b, 1)
             new_grouped(2 * b + 3)
@@ -281,6 +278,7 @@ def tile_spatialcgnl_pa_t_kernel(tc, x, Wt, Wp, Wg, out):
             pg_sum(b, 1)
             mm_pg_c0(b + 1)
             att_ps = att_mm(b)
+            mm_t(b, 1)
             rg_s(2 * b + 3)
             new_grouped(2 * b + 4)
             rg_v(2 * b + 4)
@@ -323,6 +321,16 @@ def tile_spatialcgnl_pa_t_kernel(tc, x, Wt, Wp, Wg, out):
         att_ps = att_mm(7)
         mm_t(7, 1)
         att_copy(7, att_ps)
-        t_out(7, 0, False)
-        t_out(7, 1, True)
-        store(7)
+        o_sb[7] = wrk.tile([P, HW], F32, name="o_sb", tag="o_sb")
+        for part in range(2):
+            for h in range(HALVES):
+                lo = part * (N_TILE // 2)
+                hi = lo + N_TILE // 2
+                dst = o_sb[7][:, h * N_TILE + lo : h * N_TILE + hi]
+                if h == 1:
+                    nc.vector.tensor_scalar_mul(out=dst, in0=t_ps[7, h][:, lo:hi], scalar1=att_sb[7][:, 0:1])
+                else:
+                    nc.scalar.activation(out=dst, in_=t_ps[7, h][:, lo:hi], func=ACT.Copy, scale=att_sb[7][:, 0:1])
+            for h in range(HALVES):
+                cols = slice(h * N_TILE + part * (N_TILE // 2), h * N_TILE + (part + 1) * (N_TILE // 2))
+                nc.sync.dma_start(out=ov[7][:, cols], in_=o_sb[7][:, cols])

@@ -27,7 +27,7 @@ GROUP = 16
 FLOPS = 2 * IMAGES * 3 * P * K * HW
 
 PIN = True
-V_COLS = [592, 592, 592, 464, 496, 600, 600, 600, 600, 600, 600, 600, 600, 704, 576, 592]
+V_COLS = [600, 600, 600, 600, 600, 600, 600, 600, 600, 600, 600, 600, 600, 600, 600, 512]
 
 
 def tile_spatialcgnl_pa_t_kernel(tc, x, Wt, Wp, Wg, out):
@@ -38,7 +38,7 @@ def tile_spatialcgnl_pa_t_kernel(tc, x, Wt, Wp, Wg, out):
     with ExitStack() as ctx:
         const = ctx.enter_context(tc.tile_pool(name="const", bufs=1))
         rawp = ctx.enter_context(tc.tile_pool(name="rawp", bufs=CHUNKS))
-        grpp = ctx.enter_context(tc.tile_pool(name="grpp", bufs=3))
+        grpp = ctx.enter_context(tc.tile_pool(name="grpp", bufs=4))
         codp = ctx.enter_context(tc.tile_pool(name="codp", bufs=4))
         wrk = ctx.enter_context(tc.tile_pool(name="wrk", bufs=3))
         psum = ctx.enter_context(tc.psum_pool(name="psum", bufs=2))
@@ -265,24 +265,29 @@ def tile_spatialcgnl_pa_t_kernel(tc, x, Wt, Wp, Wg, out):
         new_grouped(2)
         rg_v(2)
         rg_s(2)
+        new_grouped(3)
+        rg_s(3)
 
         for b in range(IMAGES - 2):
             mm_pg_c1(b)
             mm_t(b, 0)
             p_copy(b, 0)
             p_copy(b, 1)
-            new_grouped(2 * b + 3)
             rg_v(2 * b + 3)
             quant(2 * b + 2)
+            p_c0(b + 1, 0)
+            p_c0(b + 1, 1)
+            mm_t(b, 1)
+            new_grouped(2 * b + 4)
+            rg_s(2 * b + 4)
+            rg_v(2 * b + 4)
             pg_sum(b, 0)
             pg_sum(b, 1)
-            mm_pg_c0(b + 1)
+            g_c0(b + 1, 0)
+            g_c0(b + 1, 1)
             att_ps = att_mm(b)
-            mm_t(b, 1)
-            rg_s(2 * b + 3)
-            new_grouped(2 * b + 4)
-            rg_v(2 * b + 4)
-            rg_s(2 * b + 4)
+            new_grouped(2 * b + 5)
+            rg_s(2 * b + 5)
             att_copy(b, att_ps)
             t_out(b, 0, False)
             t_out(b, 1, False)
@@ -292,9 +297,7 @@ def tile_spatialcgnl_pa_t_kernel(tc, x, Wt, Wp, Wg, out):
         mm_pg_c1(6)
         mm_t(6, 0)
         mm_t(6, 1)
-        new_grouped(15)
         rg_v(15)
-        rg_s(15)
         p_copy(6, 0)
         p_copy(6, 1)
         quant(14)

@@ -27,6 +27,9 @@ GROUP = 16
 FLOPS = 2 * IMAGES * 3 * P * K * HW
 
 PIN = True
+G_V_COLS = 504
+G_OVERLAP = 8
+G_COLS = 160
 V_COLS = [600, 600, 600, 600, 600, 600, 600, 600, 600, 600, 600, 600, 600, 600, 600, 512]
 
 
@@ -62,20 +65,20 @@ def tile_spatialcgnl_pa_t_kernel(tc, x, Wt, Wp, Wg, out):
         att_sb = {}
         o_sb = {}
 
-        def pieces(n):
-            return [(0, HW)]
+        def has_g(n):
+            return n >= 4 and n % 2 == 0
 
-        def split(n, w0, w1):
-            v = (w1 - w0) * V_COLS[n] // HW
-            v = v - v % 8
-            return w0 + v
+        def v_end(n):
+            return G_V_COLS if has_g(n) else V_COLS[n]
+
+        def s_start(n):
+            return G_V_COLS - G_OVERLAP + G_COLS if has_g(n) else V_COLS[n]
 
         def load(n):
             b, c = divmod(n, PASSES)
             raw[n] = rawp.tile([P, PACK, HW], BF16, name="raw", tag="raw")
             src = xv[b, c * K_PASS : (c + 1) * K_PASS, :].rearrange("(p j) n -> p j n", j=PACK)
-            for w0, w1 in pieces(n):
-                nc.sync.dma_start(out=raw[n][:, :, w0:w1], in_=src[:, :, w0:w1])
+            nc.sync.dma_start(out=raw[n][:], in_=src)
 
         def regroup_views(n, w0, w1):
             dst = grouped[n][:, w0:w1, :].rearrange("p (c i) t -> p c t i", i=4)
@@ -86,14 +89,24 @@ def tile_spatialcgnl_pa_t_kernel(tc, x, Wt, Wp, Wg, out):
             grouped[n] = grpp.tile([P, HW, PACK], BF16, name="grouped", tag="grouped", align_bytes=64)
 
         def rg_v(n):
-            for w0, w1 in pieces(n):
-                dst, src = regroup_views(n, w0, split(n, w0, w1))
-                nc.vector.tensor_copy(out=dst, in_=src)
+            dst, src = regroup_views(n, 0, v_end(n))
+            nc.vector.tensor_copy(out=dst, in_=src)
 
         def rg_s(n):
-            for w0, w1 in pieces(n):
-                dst, src = regroup_views(n, split(n, w0, w1), w1)
-                nc.scalar.copy(out=dst, in_=src)
+            dst, src = regroup_views(n, s_start(n), HW)
+            nc.scalar.copy(out=dst, in_=src)
+
+        def rg_g(n):
+            w0 = G_V_COLS - G_OVERLAP
+            w1 = w0 + G_COLS
+            nc.gpsimd.tensor_scalar(
+                out=grouped[n][:, w0:w1, :],
+                in0=raw[n][:, :, w0:w1].rearrange("p t c -> p c t"),
+                scalar1=1.0,
+                scalar2=0.0,
+                op0=ALU.mult,
+                op1=ALU.add,
+            )
 
         def quant(n, w0=0, w1=HW):
             if w0 == 0:
@@ -281,6 +294,7 @@ def tile_spatialcgnl_pa_t_kernel(tc, x, Wt, Wp, Wg, out):
             new_grouped(2 * b + 4)
             rg_s(2 * b + 4)
             rg_v(2 * b + 4)
+            rg_g(2 * b + 4)
             pg_sum(b, 0)
             pg_sum(b, 1)
             g_c0(b + 1, 0)

@@ -27,10 +27,12 @@ GROUP = 16
 FLOPS = 2 * IMAGES * 3 * P * K * HW
 
 PIN = True
-G_V_COLS = 504
+G_V_COLS = 416
 G_OVERLAP = 8
 G_COLS = 160
-V_COLS = [600, 600, 600, 600, 600, 600, 600, 600, 600, 600, 600, 600, 600, 600, 600, 512]
+V_COLS = [496] * 15 + [432]
+PE_COLS = 256
+SV_COLS = HW - PE_COLS
 
 
 def tile_spatialcgnl_pa_t_kernel(tc, x, Wt, Wp, Wg, out):
@@ -52,6 +54,7 @@ def tile_spatialcgnl_pa_t_kernel(tc, x, Wt, Wp, Wg, out):
         grouped = {}
         codes = {}
         scales = {}
+        rg_ps = {}
         w_raw = {}
         w_ps = {}
         w_grp = {}
@@ -93,8 +96,25 @@ def tile_spatialcgnl_pa_t_kernel(tc, x, Wt, Wp, Wg, out):
             nc.vector.tensor_copy(out=dst, in_=src)
 
         def rg_s(n):
-            dst, src = regroup_views(n, s_start(n), HW)
+            dst, src = regroup_views(n, s_start(n), SV_COLS)
             nc.scalar.copy(out=dst, in_=src)
+
+        def rg_pe(n):
+            rg_ps[n] = psum.tile([P, PE_COLS * PACK], BF16, name="rg_ps", tag="p")
+            for q in range(PE_COLS // P):
+                c0 = SV_COLS + q * P
+                nc.tensor.matmul(
+                    rg_ps[n][:, q * N_TILE : (q + 1) * N_TILE].rearrange("p (c t) -> p t c", t=PACK),
+                    lhsT=ident_bf[:],
+                    rhs=raw[n][:, :, c0 : c0 + P],
+                    start=True,
+                    stop=True,
+                )
+
+        def rg_out(n):
+            nc.scalar.copy(
+                out=grouped[n][:, SV_COLS:HW, :].rearrange("p c t -> p (c t)"), in_=rg_ps[n][:]
+            )
 
         def rg_g(n):
             w0 = G_V_COLS - G_OVERLAP
@@ -146,14 +166,11 @@ def tile_spatialcgnl_pa_t_kernel(tc, x, Wt, Wp, Wg, out):
         def g_c1(b, h):
             mx(g_ps[b, h], "g", b, 1, h, False, True)
 
-        def mm_pg_c0(b):
+        def mm_pg(b):
             for h in range(HALVES):
                 p_c0(b, h)
-                g_c0(b, h)
-
-        def mm_pg_c1(b):
-            for h in range(HALVES):
                 p_c1(b, h)
+            for h in range(HALVES):
                 g_c1(b, h)
 
         def mm_t(b, h):
@@ -237,6 +254,8 @@ def tile_spatialcgnl_pa_t_kernel(tc, x, Wt, Wp, Wg, out):
         nc.scalar.activation(out=warm_out[:], in_=warm_in[:], func=ACT.Copy)
         ident = const.tile([P, P], F32, name="ident")
         make_identity(nc, ident[:])
+        ident_bf = const.tile([P, P], BF16, name="ident_bf")
+        make_identity(nc, ident_bf[:])
 
         w_base = {"p": 0, "g": PASSES * P, "t": 0}
         pg_grp = const.tile([P, 2 * PASSES * P * PACK], BF16, name="pg_grp", align_bytes=64)
@@ -254,18 +273,23 @@ def tile_spatialcgnl_pa_t_kernel(tc, x, Wt, Wp, Wg, out):
         w_scales["t"] = t_scales
 
         new_grouped(0)
+        rg_pe(0)
         rg_v(0)
         rg_s(0)
+        rg_out(0)
         w_transpose("p")
         w_transpose("g")
         w_copy("p")
         w_copy("g")
         quant(0)
         w_quant("p")
-        mm_pg_c0(0)
         new_grouped(1)
+        rg_pe(1)
+        g_c0(0, 0)
+        g_c0(0, 1)
         rg_v(1)
         rg_s(1)
+        rg_out(1)
         w_transpose("t")
         w_copy("t")
         grp8 = const.tile([P, P // GROUP], F32, name="grp8")
@@ -276,39 +300,45 @@ def tile_spatialcgnl_pa_t_kernel(tc, x, Wt, Wp, Wg, out):
         quant(1)
         w_quant("t")
         new_grouped(2)
+        rg_pe(2)
         rg_v(2)
         rg_s(2)
+        rg_out(2)
         new_grouped(3)
+        rg_pe(3)
         rg_s(3)
+        rg_out(3)
 
         for b in range(IMAGES - 2):
-            mm_pg_c1(b)
+            mm_pg(b)
             mm_t(b, 0)
             p_copy(b, 0)
             p_copy(b, 1)
             rg_v(2 * b + 3)
             quant(2 * b + 2)
-            p_c0(b + 1, 0)
-            p_c0(b + 1, 1)
+            rg_pe(2 * b + 4)
+            rg_pe(2 * b + 5)
             mm_t(b, 1)
             new_grouped(2 * b + 4)
             rg_s(2 * b + 4)
             rg_v(2 * b + 4)
             rg_g(2 * b + 4)
+            new_grouped(2 * b + 5)
+            rg_s(2 * b + 5)
+            rg_out(2 * b + 4)
+            rg_out(2 * b + 5)
             pg_sum(b, 0)
             pg_sum(b, 1)
             g_c0(b + 1, 0)
             g_c0(b + 1, 1)
             att_ps = att_mm(b)
-            new_grouped(2 * b + 5)
-            rg_s(2 * b + 5)
             att_copy(b, att_ps)
             t_out(b, 0, False)
             t_out(b, 1, False)
             store(b)
             quant(2 * b + 3)
 
-        mm_pg_c1(6)
+        mm_pg(6)
         mm_t(6, 0)
         mm_t(6, 1)
         rg_v(15)

@@ -27,12 +27,12 @@ GROUP = 16
 FLOPS = 2 * IMAGES * 3 * P * K * HW
 
 PIN = True
-G_V_COLS = 416
-G_OVERLAP = 8
-G_COLS = 160
-V_COLS = [496] * 15 + [432]
 PE_COLS = 256
 SV_COLS = HW - PE_COLS
+HEAD_CHUNKS = 4
+HEAD_V = 480
+ODD_V = 416
+G_OVERLAP = 8
 
 
 def tile_spatialcgnl_pa_t_kernel(tc, x, Wt, Wp, Wg, out):
@@ -68,14 +68,11 @@ def tile_spatialcgnl_pa_t_kernel(tc, x, Wt, Wp, Wg, out):
         att_sb = {}
         o_sb = {}
 
-        def has_g(n):
-            return n >= 4 and n % 2 == 0
-
         def v_end(n):
-            return G_V_COLS if has_g(n) else V_COLS[n]
+            return HEAD_V if n < HEAD_CHUNKS else ODD_V
 
         def s_start(n):
-            return G_V_COLS - G_OVERLAP + G_COLS if has_g(n) else V_COLS[n]
+            return HEAD_V if n < HEAD_CHUNKS else 0
 
         def load(n):
             b, c = divmod(n, PASSES)
@@ -112,13 +109,15 @@ def tile_spatialcgnl_pa_t_kernel(tc, x, Wt, Wp, Wg, out):
                 )
 
         def rg_out(n):
-            nc.scalar.copy(
-                out=grouped[n][:, SV_COLS:HW, :].rearrange("p c t -> p (c t)"), in_=rg_ps[n][:]
-            )
+            dst = grouped[n][:, SV_COLS:HW, :].rearrange("p c t -> p (c t)")
+            if n < HEAD_CHUNKS:
+                nc.scalar.copy(out=dst, in_=rg_ps[n][:])
+            else:
+                nc.vector.tensor_copy(out=dst, in_=rg_ps[n][:])
 
         def rg_g(n):
-            w0 = G_V_COLS - G_OVERLAP
-            w1 = w0 + G_COLS
+            w0 = ODD_V - G_OVERLAP
+            w1 = SV_COLS
             nc.gpsimd.tensor_scalar(
                 out=grouped[n][:, w0:w1, :],
                 in0=raw[n][:, :, w0:w1].rearrange("p t c -> p c t"),
@@ -156,22 +155,27 @@ def tile_spatialcgnl_pa_t_kernel(tc, x, Wt, Wp, Wg, out):
             p_ps[b, h] = psum.tile([P, N_TILE], F32, name="p_ps", tag="p")
             mx(p_ps[b, h], "p", b, 0, h, True, False)
 
-        def g_c0(b, h):
+        def g_open(b, h, c):
             g_ps[b, h] = psum.tile([P, N_TILE], F32, name="g_ps", tag="g")
-            mx(g_ps[b, h], "g", b, 0, h, True, False)
+            mx(g_ps[b, h], "g", b, c, h, True, False)
+
+        def g_close(b, h, c):
+            mx(g_ps[b, h], "g", b, c, h, False, True)
+
+        def p_c1_first(b, h):
+            p_ps[b, h] = psum.tile([P, N_TILE], F32, name="p_ps", tag="p")
+            mx(p_ps[b, h], "p", b, 1, h, True, False)
+            mx(p_ps[b, h], "p", b, 0, h, False, True)
 
         def p_c1(b, h):
             mx(p_ps[b, h], "p", b, 1, h, False, True)
 
-        def g_c1(b, h):
-            mx(g_ps[b, h], "g", b, 1, h, False, True)
-
-        def mm_pg(b):
+        def mm_pg(b, c_last):
             for h in range(HALVES):
                 p_c0(b, h)
                 p_c1(b, h)
             for h in range(HALVES):
-                g_c1(b, h)
+                g_close(b, h, c_last)
 
         def mm_t(b, h):
             t_ps[b, h] = psum.tile([P, N_TILE], F32, name="t_ps", tag="t", bufs=3)
@@ -285,8 +289,8 @@ def tile_spatialcgnl_pa_t_kernel(tc, x, Wt, Wp, Wg, out):
         w_quant("p")
         new_grouped(1)
         rg_pe(1)
-        g_c0(0, 0)
-        g_c0(0, 1)
+        g_open(0, 0, 0)
+        g_open(0, 1, 0)
         rg_v(1)
         rg_s(1)
         rg_out(1)
@@ -307,62 +311,63 @@ def tile_spatialcgnl_pa_t_kernel(tc, x, Wt, Wp, Wg, out):
         new_grouped(3)
         rg_pe(3)
         rg_s(3)
+        rg_v(3)
         rg_out(3)
 
-        for b in range(IMAGES - 2):
-            mm_pg(b)
-            mm_t(b, 0)
-            p_copy(b, 0)
-            p_copy(b, 1)
-            rg_v(2 * b + 3)
-            quant(2 * b + 2)
-            rg_pe(2 * b + 4)
-            rg_pe(2 * b + 5)
-            mm_t(b, 1)
-            new_grouped(2 * b + 4)
-            rg_s(2 * b + 4)
-            rg_v(2 * b + 4)
-            rg_g(2 * b + 4)
-            new_grouped(2 * b + 5)
-            rg_s(2 * b + 5)
-            rg_out(2 * b + 4)
-            rg_out(2 * b + 5)
-            pg_sum(b, 0)
-            pg_sum(b, 1)
-            g_c0(b + 1, 0)
-            g_c0(b + 1, 1)
-            att_ps = att_mm(b)
-            att_copy(b, att_ps)
+        att_tiles = {}
+
+        def finish(b):
+            att_copy(b, att_tiles[b])
             t_out(b, 0, False)
             t_out(b, 1, False)
             store(b)
-            quant(2 * b + 3)
 
-        mm_pg(6)
-        mm_t(6, 0)
-        mm_t(6, 1)
-        rg_v(15)
+        for b in range(IMAGES - 2):
+            mm_pg(b, 1 if b == 0 else 0)
+            p_copy(b, 0)
+            p_copy(b, 1)
+            if b > 0:
+                finish(b - 1)
+            quant(2 * b + 3)
+            rg_pe(2 * b + 4)
+            rg_pe(2 * b + 5)
+            new_grouped(2 * b + 4)
+            rg_s(2 * b + 4)
+            new_grouped(2 * b + 5)
+            rg_v(2 * b + 5)
+            rg_g(2 * b + 5)
+            pg_sum(b, 0)
+            pg_sum(b, 1)
+            att_tiles[b] = att_mm(b)
+            mm_t(b, 0)
+            mm_t(b, 1)
+            g_open(b + 1, 0, 1)
+            g_open(b + 1, 1, 1)
+            rg_out(2 * b + 4)
+            rg_out(2 * b + 5)
+            quant(2 * b + 2)
+
+        mm_pg(6, 0)
         p_copy(6, 0)
         p_copy(6, 1)
-        quant(14)
-        quant(15, 0, N_TILE)
-        quant(15, N_TILE, HW)
+        finish(5)
+        quant(15)
+        quant(14, 0, N_TILE)
+        quant(14, N_TILE, HW)
         pg_sum(6, 0)
         pg_sum(6, 1)
+        mm_t(6, 0)
+        mm_t(6, 1)
         for h in range(HALVES):
-            p_c0(7, h)
-            p_c1(7, h)
+            p_c1_first(7, h)
         for h in range(HALVES):
-            g_c0(7, h)
-            g_c1(7, h)
-        att_ps = att_mm(6)
+            g_open(7, h, 1)
+            g_close(7, h, 0)
+        att_tiles[6] = att_mm(6)
         mm_t(7, 0)
         p_copy(7, 0)
         p_copy(7, 1)
-        att_copy(6, att_ps)
-        t_out(6, 0, False)
-        t_out(6, 1, False)
-        store(6)
+        finish(6)
         pg_sum(7, 0)
         pg_sum(7, 1)
         att_ps = att_mm(7)

@@ -109,11 +109,11 @@ def tile_spatialcgnl_pa_t_kernel(tc, x, Wt, Wp, Wg, out):
                 )
 
         def rg_out(n):
-            dst = grouped[n][:, SV_COLS:HW, :].rearrange("p c t -> p (c t)")
+            dst = grouped[n][:, SV_COLS:HW, :].rearrange("p c t -> p (c t)").bitcast(F32)
             if n < HEAD_CHUNKS:
-                nc.scalar.copy(out=dst, in_=rg_ps[n][:])
+                nc.scalar.copy(out=dst, in_=rg_ps[n][:].bitcast(F32))
             else:
-                nc.vector.tensor_copy(out=dst, in_=rg_ps[n][:])
+                nc.vector.tensor_copy(out=dst, in_=rg_ps[n][:].bitcast(F32))
 
         def rg_g(n):
             w0 = ODD_V - G_OVERLAP

@@ -33,6 +33,7 @@ HEAD_CHUNKS = 4
 HEAD_V = 480
 ODD_V = 416
 G_OVERLAP = 8
+O_BUFS = 6
 
 
 def tile_spatialcgnl_pa_t_kernel(tc, x, Wt, Wp, Wg, out):
@@ -162,11 +163,6 @@ def tile_spatialcgnl_pa_t_kernel(tc, x, Wt, Wp, Wg, out):
         def g_close(b, h, c):
             mx(g_ps[b, h], "g", b, c, h, False, True)
 
-        def p_c1_first(b, h):
-            p_ps[b, h] = psum.tile([P, N_TILE], F32, name="p_ps", tag="p")
-            mx(p_ps[b, h], "p", b, 1, h, True, False)
-            mx(p_ps[b, h], "p", b, 0, h, False, True)
-
         def p_c1(b, h):
             mx(p_ps[b, h], "p", b, 1, h, False, True)
 
@@ -212,7 +208,7 @@ def tile_spatialcgnl_pa_t_kernel(tc, x, Wt, Wp, Wg, out):
 
         def t_out(b, h, on_vector):
             if h == 0:
-                o_sb[b] = wrk.tile([P, HW], F32, name="o_sb", tag="o_sb")
+                o_sb[b] = wrk.tile([P, HW], F32, name="o_sb", tag="o_sb", bufs=O_BUFS)
             dst = o_sb[b][:, h * N_TILE : (h + 1) * N_TILE]
             if on_vector:
                 nc.vector.tensor_scalar_mul(out=dst, in0=t_ps[b, h][:], scalar1=att_sb[b][:, 0:1])
@@ -323,46 +319,47 @@ def tile_spatialcgnl_pa_t_kernel(tc, x, Wt, Wp, Wg, out):
             store(b)
 
         for b in range(IMAGES - 2):
-            mm_pg(b, 1 if b == 0 else 0)
+            mm_pg(b, 1)
             p_copy(b, 0)
             p_copy(b, 1)
             if b > 0:
                 finish(b - 1)
-            quant(2 * b + 3)
+            quant(2 * b + 2)
             rg_pe(2 * b + 4)
             rg_pe(2 * b + 5)
             new_grouped(2 * b + 4)
-            rg_s(2 * b + 4)
+            rg_v(2 * b + 4)
+            rg_g(2 * b + 4)
             new_grouped(2 * b + 5)
-            rg_v(2 * b + 5)
-            rg_g(2 * b + 5)
+            rg_s(2 * b + 5)
             pg_sum(b, 0)
             pg_sum(b, 1)
             att_tiles[b] = att_mm(b)
             mm_t(b, 0)
             mm_t(b, 1)
-            g_open(b + 1, 0, 1)
-            g_open(b + 1, 1, 1)
+            g_open(b + 1, 0, 0)
+            g_open(b + 1, 1, 0)
             rg_out(2 * b + 4)
             rg_out(2 * b + 5)
-            quant(2 * b + 2)
+            quant(2 * b + 3)
 
-        mm_pg(6, 0)
+        mm_pg(6, 1)
         p_copy(6, 0)
         p_copy(6, 1)
         finish(5)
-        quant(15)
         quant(14, 0, N_TILE)
+        quant(15, 0, N_TILE)
         quant(14, N_TILE, HW)
+        quant(15, N_TILE, HW)
         pg_sum(6, 0)
         pg_sum(6, 1)
         mm_t(6, 0)
         mm_t(6, 1)
         for h in range(HALVES):
-            p_c1_first(7, h)
-        for h in range(HALVES):
-            g_open(7, h, 1)
-            g_close(7, h, 0)
+            p_c0(7, h)
+            p_c1(7, h)
+            g_open(7, h, 0)
+            g_close(7, h, 1)
         att_tiles[6] = att_mm(6)
         mm_t(7, 0)
         p_copy(7, 0)
@@ -373,7 +370,7 @@ def tile_spatialcgnl_pa_t_kernel(tc, x, Wt, Wp, Wg, out):
         att_ps = att_mm(7)
         mm_t(7, 1)
         att_copy(7, att_ps)
-        o_sb[7] = wrk.tile([P, HW], F32, name="o_sb", tag="o_sb")
+        o_sb[7] = wrk.tile([P, HW], F32, name="o_sb", tag="o_sb", bufs=O_BUFS)
         for part in range(2):
             for h in range(HALVES):
                 lo = part * (N_TILE // 2)

@@ -31,7 +31,7 @@ PE_COLS = 256
 SV_COLS = HW - PE_COLS
 HEAD_CHUNKS = 4
 HEAD_V = 480
-ODD_V = 416
+ODD_V = 384
 G_OVERLAP = 8
 O_BUFS = 6
 
@@ -173,13 +173,13 @@ def tile_spatialcgnl_pa_t_kernel(tc, x, Wt, Wp, Wg, out):
             for h in range(HALVES):
                 g_close(b, h, c_last)
 
-        def mm_t(b, h):
-            t_ps[b, h] = psum.tile([P, N_TILE], F32, name="t_ps", tag="t", bufs=3)
+        def mm_t(b, h, tag="t"):
+            t_ps[b, h] = psum.tile([P, N_TILE], F32, name="t_ps", tag=tag, bufs=3 if tag == "t" else 2)
             mx(t_ps[b, h], "t", b, 0, h, True, False)
             mx(t_ps[b, h], "t", b, 1, h, False, True)
 
         def p_copy(b, h):
-            p_sb[b, h] = wrk.tile([P, N_TILE], F32, name="p_sb", tag="p_sb")
+            p_sb[b, h] = wrk.tile([P, N_TILE], F32, name="p_sb", tag="p_sb", bufs=4)
             nc.scalar.copy(out=p_sb[b, h][:], in_=p_ps[b, h][:])
 
         def pg_sum(b, h):
@@ -254,6 +254,11 @@ def tile_spatialcgnl_pa_t_kernel(tc, x, Wt, Wp, Wg, out):
         nc.scalar.activation(out=warm_out[:], in_=warm_in[:], func=ACT.Copy)
         ident = const.tile([P, P], F32, name="ident")
         make_identity(nc, ident[:])
+        grp8 = const.tile([P, P // GROUP], F32, name="grp8")
+        nc.vector.reduce_sum(out=grp8[:], in_=ident[:].rearrange("p (j i) -> p j i", i=GROUP), axis=AX.X)
+        blk = const.tile([P, P // GROUP, GROUP], F32, name="blk")
+        nc.vector.tensor_copy(out=blk[:], in_=grp8[:].unsqueeze(2).to_broadcast([P, P // GROUP, GROUP]))
+        blk2d = blk[:].rearrange("p j i -> p (j i)")
         ident_bf = const.tile([P, P], BF16, name="ident_bf")
         make_identity(nc, ident_bf[:])
 
@@ -292,11 +297,6 @@ def tile_spatialcgnl_pa_t_kernel(tc, x, Wt, Wp, Wg, out):
         rg_out(1)
         w_transpose("t")
         w_copy("t")
-        grp8 = const.tile([P, P // GROUP], F32, name="grp8")
-        nc.vector.reduce_sum(out=grp8[:], in_=ident[:].rearrange("p (j i) -> p j i", i=GROUP), axis=AX.X)
-        blk = const.tile([P, P // GROUP, GROUP], F32, name="blk")
-        nc.vector.tensor_copy(out=blk[:], in_=grp8[:].unsqueeze(2).to_broadcast([P, P // GROUP, GROUP]))
-        blk2d = blk[:].rearrange("p j i -> p (j i)")
         quant(1)
         w_quant("t")
         new_grouped(2)
@@ -343,32 +343,33 @@ def tile_spatialcgnl_pa_t_kernel(tc, x, Wt, Wp, Wg, out):
             rg_out(2 * b + 5)
             quant(2 * b + 3)
 
+        finish(5)
         mm_pg(6, 1)
+        mm_t(6, 0)
+        mm_t(6, 1)
         p_copy(6, 0)
         p_copy(6, 1)
-        finish(5)
         quant(14, 0, N_TILE)
         quant(15, 0, N_TILE)
         quant(14, N_TILE, HW)
         quant(15, N_TILE, HW)
-        pg_sum(6, 0)
-        pg_sum(6, 1)
-        mm_t(6, 0)
-        mm_t(6, 1)
         for h in range(HALVES):
             p_c0(7, h)
             p_c1(7, h)
+        p_copy(7, 0)
+        p_copy(7, 1)
+        pg_sum(6, 0)
+        pg_sum(6, 1)
+        for h in range(HALVES):
             g_open(7, h, 0)
             g_close(7, h, 1)
         att_tiles[6] = att_mm(6)
         mm_t(7, 0)
-        p_copy(7, 0)
-        p_copy(7, 1)
+        mm_t(7, 1, "p")
         finish(6)
         pg_sum(7, 0)
         pg_sum(7, 1)
         att_ps = att_mm(7)
-        mm_t(7, 1)
         att_copy(7, att_ps)
         o_sb[7] = wrk.tile([P, HW], F32, name="o_sb", tag="o_sb", bufs=O_BUFS)
         for part in range(2):

@@ -31,7 +31,7 @@ PE_COLS = 256
 SV_COLS = HW - PE_COLS
 HEAD_CHUNKS = 4
 HEAD_V = 480
-ODD_V = 384
+ODD_V = 352
 G_OVERLAP = 8
 O_BUFS = 6
 

@@ -313,13 +313,14 @@ def tile_spatialcgnl_pa_t_kernel(tc, x, Wt, Wp, Wg, out):
         att_tiles = {}
 
         def finish(b):
-            att_copy(b, att_tiles[b])
             t_out(b, 0, False)
             t_out(b, 1, False)
             store(b)
 
         for b in range(IMAGES - 2):
             mm_pg(b, 1)
+            if b > 0:
+                att_copy(b - 1, att_tiles[b - 1])
             p_copy(b, 0)
             p_copy(b, 1)
             if b > 0:
@@ -343,12 +344,13 @@ def tile_spatialcgnl_pa_t_kernel(tc, x, Wt, Wp, Wg, out):
             rg_out(2 * b + 5)
             quant(2 * b + 3)
 
-        finish(5)
+        att_copy(5, att_tiles[5])
         mm_pg(6, 1)
         mm_t(6, 0)
         mm_t(6, 1)
         p_copy(6, 0)
         p_copy(6, 1)
+        finish(5)
         quant(14, 0, N_TILE)
         quant(15, 0, N_TILE)
         quant(14, N_TILE, HW)
@@ -366,6 +368,7 @@ def tile_spatialcgnl_pa_t_kernel(tc, x, Wt, Wp, Wg, out):
         att_tiles[6] = att_mm(6)
         mm_t(7, 0)
         mm_t(7, 1, "p")
+        att_copy(6, att_tiles[6])
         finish(6)
         pg_sum(7, 0)
         pg_sum(7, 1)

@@ -277,6 +277,15 @@ def tile_spatialcgnl_pa_t_kernel(tc, x, Wt, Wp, Wg, out):
         w_codes["t"] = t_codes
         w_scales["t"] = t_scales
 
+        zeros = const.tile([P, N_TILE], BF16, name="zeros")
+        nc.vector.memset(zeros[:], 0.0)
+        warm_ps = psum.tile([P, N_TILE], F32, name="warm_ps", tag="t", bufs=3)
+
+        def warm(count):
+            for i in range(count):
+                nc.tensor.matmul(warm_ps[:], lhsT=ident_bf[:], rhs=zeros[:], start=True, stop=True)
+
+        warm(4)
         new_grouped(0)
         rg_pe(0)
         rg_v(0)
@@ -284,6 +293,7 @@ def tile_spatialcgnl_pa_t_kernel(tc, x, Wt, Wp, Wg, out):
         rg_out(0)
         w_transpose("p")
         w_transpose("g")
+        warm(2)
         w_copy("p")
         w_copy("g")
         quant(0)
@@ -346,11 +356,11 @@ def tile_spatialcgnl_pa_t_kernel(tc, x, Wt, Wp, Wg, out):
 
         att_copy(5, att_tiles[5])
         mm_pg(6, 1)
-        mm_t(6, 0)
-        mm_t(6, 1)
         p_copy(6, 0)
         p_copy(6, 1)
         finish(5)
+        mm_t(6, 0)
+        mm_t(6, 1)
         quant(14, 0, N_TILE)
         quant(15, 0, N_TILE)
         quant(14, N_TILE, HW)

@@ -27,11 +27,12 @@ GROUP = 16
 FLOPS = 2 * IMAGES * 3 * P * K * HW
 
 PIN = True
-PE_COLS = 256
+PE_COLS = 192
+PE_Q = 96
 SV_COLS = HW - PE_COLS
 HEAD_CHUNKS = 4
-HEAD_V = 480
-ODD_V = 352
+HEAD_V = 512
+ODD_V = 416
 G_OVERLAP = 8
 O_BUFS = 6
 
@@ -99,12 +100,12 @@ def tile_spatialcgnl_pa_t_kernel(tc, x, Wt, Wp, Wg, out):
 
         def rg_pe(n):
             rg_ps[n] = psum.tile([P, PE_COLS * PACK], BF16, name="rg_ps", tag="p")
-            for q in range(PE_COLS // P):
-                c0 = SV_COLS + q * P
+            for q in range(PE_COLS // PE_Q):
+                c0 = SV_COLS + q * PE_Q
                 nc.tensor.matmul(
-                    rg_ps[n][:, q * N_TILE : (q + 1) * N_TILE].rearrange("p (c t) -> p t c", t=PACK),
+                    rg_ps[n][:, q * PE_Q * PACK : (q + 1) * PE_Q * PACK].rearrange("p (c t) -> p t c", t=PACK),
                     lhsT=ident_bf[:],
-                    rhs=raw[n][:, :, c0 : c0 + P],
+                    rhs=raw[n][:, :, c0 : c0 + PE_Q],
                     start=True,
                     stop=True,
                 )

@@ -27,12 +27,10 @@ GROUP = 16
 FLOPS = 2 * IMAGES * 3 * P * K * HW
 
 PIN = True
-PE_COLS = 192
-PE_Q = 96
-SV_COLS = HW - PE_COLS
+PE_COLS = (128, 256)
 HEAD_CHUNKS = 4
 HEAD_V = 512
-ODD_V = 416
+ODD_V = 480
 G_OVERLAP = 8
 O_BUFS = 6
 
@@ -70,6 +68,9 @@ def tile_spatialcgnl_pa_t_kernel(tc, x, Wt, Wp, Wg, out):
         att_sb = {}
         o_sb = {}
 
+        def pe_start(n):
+            return HW - PE_COLS[n % PASSES]
+
         def v_end(n):
             return HEAD_V if n < HEAD_CHUNKS else ODD_V
 
@@ -95,23 +96,23 @@ def tile_spatialcgnl_pa_t_kernel(tc, x, Wt, Wp, Wg, out):
             nc.vector.tensor_copy(out=dst, in_=src)
 
         def rg_s(n):
-            dst, src = regroup_views(n, s_start(n), SV_COLS)
+            dst, src = regroup_views(n, s_start(n), pe_start(n))
             nc.scalar.copy(out=dst, in_=src)
 
         def rg_pe(n):
-            rg_ps[n] = psum.tile([P, PE_COLS * PACK], BF16, name="rg_ps", tag="p")
-            for q in range(PE_COLS // PE_Q):
-                c0 = SV_COLS + q * PE_Q
+            rg_ps[n] = psum.tile([P, PE_COLS[n % PASSES] * PACK], BF16, name="rg_ps", tag="p")
+            for q in range(PE_COLS[n % PASSES] // P):
+                c0 = pe_start(n) + q * P
                 nc.tensor.matmul(
-                    rg_ps[n][:, q * PE_Q * PACK : (q + 1) * PE_Q * PACK].rearrange("p (c t) -> p t c", t=PACK),
+                    rg_ps[n][:, q * N_TILE : (q + 1) * N_TILE].rearrange("p (c t) -> p t c", t=PACK),
                     lhsT=ident_bf[:],
-                    rhs=raw[n][:, :, c0 : c0 + PE_Q],
+                    rhs=raw[n][:, :, c0 : c0 + P],
                     start=True,
                     stop=True,
                 )
 
         def rg_out(n):
-            dst = grouped[n][:, SV_COLS:HW, :].rearrange("p c t -> p (c t)").bitcast(F32)
+            dst = grouped[n][:, pe_start(n) : HW, :].rearrange("p c t -> p (c t)").bitcast(F32)
             if n < HEAD_CHUNKS:
                 nc.scalar.copy(out=dst, in_=rg_ps[n][:].bitcast(F32))
             else:
@@ -119,7 +120,7 @@ def tile_spatialcgnl_pa_t_kernel(tc, x, Wt, Wp, Wg, out):
 
         def rg_g(n):
             w0 = ODD_V - G_OVERLAP
-            w1 = SV_COLS
+            w1 = pe_start(n)
             nc.gpsimd.tensor_scalar(
                 out=grouped[n][:, w0:w1, :],
                 in0=raw[n][:, :, w0:w1].rearrange("p t c -> p c t"),
@@ -355,35 +356,38 @@ def tile_spatialcgnl_pa_t_kernel(tc, x, Wt, Wp, Wg, out):
             rg_out(2 * b + 5)
             quant(2 * b + 3)
 
-        att_copy(5, att_tiles[5])
         mm_pg(6, 1)
+        att_copy(5, att_tiles[5])
         p_copy(6, 0)
         p_copy(6, 1)
-        finish(5)
         mm_t(6, 0)
-        mm_t(6, 1)
-        quant(14, 0, N_TILE)
+        quant(14)
         quant(15, 0, N_TILE)
-        quant(14, N_TILE, HW)
-        quant(15, N_TILE, HW)
-        for h in range(HALVES):
-            p_c0(7, h)
-            p_c1(7, h)
-        p_copy(7, 0)
-        p_copy(7, 1)
         pg_sum(6, 0)
+        p_c0(7, 0)
+        p_c1(7, 0)
+        g_open(7, 0, 0)
+        g_close(7, 0, 1)
+        finish(5)
+        p_copy(7, 0)
+        quant(15, N_TILE, HW)
         pg_sum(6, 1)
-        for h in range(HALVES):
-            g_open(7, h, 0)
-            g_close(7, h, 1)
+        p_c0(7, 1)
+        p_c1(7, 1)
+        g_open(7, 1, 0)
+        g_close(7, 1, 1)
+        p_copy(7, 1)
         att_tiles[6] = att_mm(6)
-        mm_t(7, 0)
-        mm_t(7, 1, "p")
+        mm_t(6, 1)
         att_copy(6, att_tiles[6])
-        finish(6)
         pg_sum(7, 0)
         pg_sum(7, 1)
+        t_out(6, 0, False)
+        t_out(6, 1, True)
+        store(6)
+        mm_t(7, 0)
         att_ps = att_mm(7)
+        mm_t(7, 1, "p")
         att_copy(7, att_ps)
         o_sb[7] = wrk.tile([P, HW], F32, name="o_sb", tag="o_sb", bufs=O_BUFS)
         for part in range(2):

@@ -30,8 +30,9 @@ PIN = True
 PE_COLS = (128, 256)
 HEAD_CHUNKS = 4
 HEAD_V = 512
-ODD_V = 480
+ODD_V = 576
 G_OVERLAP = 8
+EVEN_S = 864
 O_BUFS = 6
 
 
@@ -95,18 +96,20 @@ def tile_spatialcgnl_pa_t_kernel(tc, x, Wt, Wp, Wg, out):
             dst, src = regroup_views(n, 0, v_end(n))
             nc.vector.tensor_copy(out=dst, in_=src)
 
-        def rg_s(n):
-            dst, src = regroup_views(n, s_start(n), pe_start(n))
+        def rg_s(n, w0=None):
+            dst, src = regroup_views(n, s_start(n) if w0 is None else w0, pe_start(n))
             nc.scalar.copy(out=dst, in_=src)
 
         def rg_pe(n):
             rg_ps[n] = psum.tile([P, PE_COLS[n % PASSES] * PACK], BF16, name="rg_ps", tag="p")
-            for q in range(PE_COLS[n % PASSES] // P):
-                c0 = pe_start(n) + q * P
+            count = -(-PE_COLS[n % PASSES] // P)
+            width = PE_COLS[n % PASSES] // count
+            for q in range(count):
+                c0 = pe_start(n) + q * width
                 nc.tensor.matmul(
-                    rg_ps[n][:, q * N_TILE : (q + 1) * N_TILE].rearrange("p (c t) -> p t c", t=PACK),
+                    rg_ps[n][:, q * width * PACK : (q + 1) * width * PACK].rearrange("p (c t) -> p t c", t=PACK),
                     lhsT=ident_bf[:],
-                    rhs=raw[n][:, :, c0 : c0 + P],
+                    rhs=raw[n][:, :, c0 : c0 + width],
                     start=True,
                     stop=True,
                 )
@@ -120,7 +123,7 @@ def tile_spatialcgnl_pa_t_kernel(tc, x, Wt, Wp, Wg, out):
 
         def rg_g(n):
             w0 = ODD_V - G_OVERLAP
-            w1 = pe_start(n)
+            w1 = EVEN_S
             nc.gpsimd.tensor_scalar(
                 out=grouped[n][:, w0:w1, :],
                 in0=raw[n][:, :, w0:w1].rearrange("p t c -> p c t"),
@@ -344,12 +347,13 @@ def tile_spatialcgnl_pa_t_kernel(tc, x, Wt, Wp, Wg, out):
             rg_v(2 * b + 4)
             rg_g(2 * b + 4)
             new_grouped(2 * b + 5)
+            rg_s(2 * b + 4, EVEN_S)
             rg_s(2 * b + 5)
             pg_sum(b, 0)
             pg_sum(b, 1)
-            att_tiles[b] = att_mm(b)
             mm_t(b, 0)
             mm_t(b, 1)
+            att_tiles[b] = att_mm(b)
             g_open(b + 1, 0, 0)
             g_open(b + 1, 1, 0)
             rg_out(2 * b + 4)

@@ -27,12 +27,12 @@ GROUP = 16
 FLOPS = 2 * IMAGES * 3 * P * K * HW
 
 PIN = True
-PE_COLS = (128, 256)
+PE_COLS = (160, 256)
 HEAD_CHUNKS = 4
 HEAD_V = 512
-ODD_V = 576
+ODD_V = 480
 G_OVERLAP = 8
-EVEN_S = 864
+EVEN_S = 832
 O_BUFS = 6
 
 
@@ -319,9 +319,12 @@ def tile_spatialcgnl_pa_t_kernel(tc, x, Wt, Wp, Wg, out):
         rg_v(2)
         rg_s(2)
         rg_out(2)
+        mm_pg(0, 1)
         new_grouped(3)
-        rg_pe(3)
         rg_s(3)
+        p_copy(0, 0)
+        p_copy(0, 1)
+        rg_pe(3)
         rg_v(3)
         rg_out(3)
 
@@ -333,12 +336,11 @@ def tile_spatialcgnl_pa_t_kernel(tc, x, Wt, Wp, Wg, out):
             store(b)
 
         for b in range(IMAGES - 2):
-            mm_pg(b, 1)
             if b > 0:
+                mm_pg(b, 1)
                 att_copy(b - 1, att_tiles[b - 1])
-            p_copy(b, 0)
-            p_copy(b, 1)
-            if b > 0:
+                p_copy(b, 0)
+                p_copy(b, 1)
                 finish(b - 1)
             quant(2 * b + 2)
             rg_pe(2 * b + 4)

from contextlib import ExitStack

import concourse.mybir as mybir
from concourse.masks import make_identity

F32 = mybir.dt.float32
BF16 = mybir.dt.bfloat16
U32 = mybir.dt.uint32
U8 = mybir.dt.uint8
FP8X4 = mybir.dt.float8_e4m3fn_x4
ALU = mybir.AluOpType
ACT = mybir.ActivationFunctionType
AX = mybir.AxisListType

IMAGES = 8
K = 1024
HW = 1024
P = 128
PACK = 4
K_PASS = P * PACK
PASSES = K // K_PASS
N_TILE = 512
HALVES = HW // N_TILE
CHUNKS = IMAGES * PASSES
GROUP = 16

FLOPS = 2 * IMAGES * 3 * P * K * HW

PIN = True
PE_COLS = (160, 256)
HEAD_CHUNKS = 4
HEAD_V = 512
ODD_V = 480
G_OVERLAP = 8
EVEN_S = 832
O_BUFS = 6


def tile_spatialcgnl_pa_t_kernel(tc, x, Wt, Wp, Wg, out):
    nc = tc.nc
    xv = x.rearrange("b k h w -> b k (h w)")
    ov = out.rearrange("b g c n -> b (g c) n")

    with ExitStack() as ctx:
        const = ctx.enter_context(tc.tile_pool(name="const", bufs=1))
        rawp = ctx.enter_context(tc.tile_pool(name="rawp", bufs=CHUNKS))
        grpp = ctx.enter_context(tc.tile_pool(name="grpp", bufs=4))
        codp = ctx.enter_context(tc.tile_pool(name="codp", bufs=4))
        wrk = ctx.enter_context(tc.tile_pool(name="wrk", bufs=3))
        psum = ctx.enter_context(tc.psum_pool(name="psum", bufs=2))
        if PIN:
            ctx.enter_context(tc.manual_schedule())

        raw = {}
        grouped = {}
        codes = {}
        scales = {}
        rg_ps = {}
        w_raw = {}
        w_ps = {}
        w_grp = {}
        w_codes = {}
        w_scales = {}
        p_ps = {}
        g_ps = {}
        t_ps = {}
        p_sb = {}
        acc = {}
        att_sb = {}
        o_sb = {}

        def pe_start(n):
            return HW - PE_COLS[n % PASSES]

        def v_end(n):
            return HEAD_V if n < HEAD_CHUNKS else ODD_V

        def s_start(n):
            return HEAD_V if n < HEAD_CHUNKS else 0

        def load(n):
            b, c = divmod(n, PASSES)
            raw[n] = rawp.tile([P, PACK, HW], BF16, name="raw", tag="raw")
            src = xv[b, c * K_PASS : (c + 1) * K_PASS, :].rearrange("(p j) n -> p j n", j=PACK)
            nc.sync.dma_start(out=raw[n][:], in_=src)

        def regroup_views(n, w0, w1):
            dst = grouped[n][:, w0:w1, :].rearrange("p (c i) t -> p c t i", i=4)
            src = raw[n][:, :, w0:w1].rearrange("p t (c i) -> p c t i", i=4)
            return dst, src

        def new_grouped(n):
            grouped[n] = grpp.tile([P, HW, PACK], BF16, name="grouped", tag="grouped", align_bytes=64)

        def rg_v(n):
            dst, src = regroup_views(n, 0, v_end(n))
            nc.vector.tensor_copy(out=dst, in_=src)

        def rg_s(n, w0=None):
            dst, src = regroup_views(n, s_start(n) if w0 is None else w0, pe_start(n))
            nc.scalar.copy(out=dst, in_=src)

        def rg_pe(n):
            rg_ps[n] = psum.tile([P, PE_COLS[n % PASSES] * PACK], BF16, name="rg_ps", tag="p")
            count = -(-PE_COLS[n % PASSES] // P)
            width = PE_COLS[n % PASSES] // count
            for q in range(count):
                c0 = pe_start(n) + q * width
                nc.tensor.matmul(
                    rg_ps[n][:, q * width * PACK : (q + 1) * width * PACK].rearrange("p (c t) -> p t c", t=PACK),
                    lhsT=ident_bf[:],
                    rhs=raw[n][:, :, c0 : c0 + width],
                    start=True,
                    stop=True,
                )

        def rg_out(n):
            dst = grouped[n][:, pe_start(n) : HW, :].rearrange("p c t -> p (c t)").bitcast(F32)
            if n < HEAD_CHUNKS:
                nc.scalar.copy(out=dst, in_=rg_ps[n][:].bitcast(F32))
            else:
                nc.vector.tensor_copy(out=dst, in_=rg_ps[n][:].bitcast(F32))

        def rg_g(n):
            w0 = ODD_V - G_OVERLAP
            w1 = EVEN_S
            nc.gpsimd.tensor_scalar(
                out=grouped[n][:, w0:w1, :],
                in0=raw[n][:, :, w0:w1].rearrange("p t c -> p c t"),
                scalar1=1.0,
                scalar2=0.0,
                op0=ALU.mult,
                op1=ALU.add,
            )

        def quant(n, w0=0, w1=HW):
            if w0 == 0:
                codes[n] = codp.tile([P, HW], U32, name="codes", tag="codes", align_bytes=64)
                scales[n] = codp.tile([P, HW], U8, name="scales", tag="scales", align_bytes=64)
            nc.vector.quantize_mx(
                out=codes[n][:, w0:w1].bitcast(FP8X4),
                scales=scales[n][:, w0:w1],
                in_=grouped[n][:, w0:w1, :].rearrange("p w j -> p (w j)"),
            )

        def mx(acc_ps, w, b, c, h, start, stop):
            n = b * PASSES + c
            m_cols = slice(w_base[w] + c * P, w_base[w] + (c + 1) * P)
            n_cols = slice(h * N_TILE, (h + 1) * N_TILE)
            nc.tensor.matmul_mx(
                out=acc_ps[:],
                lhsT=w_codes[w][:, m_cols].bitcast(FP8X4),
                lhsT_scale=w_scales[w][:, m_cols],
                rhs=codes[n][:, n_cols].bitcast(FP8X4),
                rhs_scale=scales[n][:, n_cols],
                start=start,
                stop=stop,
            )

        def p_c0(b, h):
            p_ps[b, h] = psum.tile([P, N_TILE], F32, name="p_ps", tag="p")
            mx(p_ps[b, h], "p", b, 0, h, True, False)

        def g_open(b, h, c):
            g_ps[b, h] = psum.tile([P, N_TILE], F32, name="g_ps", tag="g")
            mx(g_ps[b, h], "g", b, c, h, True, False)

        def g_close(b, h, c):
            mx(g_ps[b, h], "g", b, c, h, False, True)

        def p_c1(b, h):
            mx(p_ps[b, h], "p", b, 1, h, False, True)

        def mm_pg(b, c_last):
            for h in range(HALVES):
                p_c0(b, h)
                p_c1(b, h)
            for h in range(HALVES):
                g_close(b, h, c_last)

        def mm_t(b, h, tag="t"):
            t_ps[b, h] = psum.tile([P, N_TILE], F32, name="t_ps", tag=tag, bufs=3 if tag == "t" else 2)
            mx(t_ps[b, h], "t", b, 0, h, True, False)
            mx(t_ps[b, h], "t", b, 1, h, False, True)

        def p_copy(b, h):
            p_sb[b, h] = wrk.tile([P, N_TILE], F32, name="p_sb", tag="p_sb", bufs=4)
            nc.scalar.copy(out=p_sb[b, h][:], in_=p_ps[b, h][:])

        def pg_sum(b, h):
            if h == 0:
                acc[b] = wrk.tile([P, HALVES], F32, name="acc", tag="acc")
            junk = wrk.tile([P, N_TILE], F32, name="junk", tag="junk", bufs=2)
            nc.vector.scalar_tensor_tensor(
                out=junk[:],
                in0=g_ps[b, h][:],
                scalar=1.0,
                in1=p_sb[b, h][:],
                op0=ALU.mult,
                op1=ALU.mult,
                accum_out=acc[b][:, h : h + 1],
            )

        def att_mm(b):
            att_ps = psum.tile([P, HALVES], F32, name="att_ps", tag="att", bufs=1)
            nc.tensor.matmul(att_ps[:], lhsT=blk2d, rhs=acc[b][:], start=True, stop=True)
            return att_ps

        def att_copy(b, att_ps):
            att_sb[b] = wrk.tile([P, 1], F32, name="att_sb", tag="att_sb")
            att_junk = wrk.tile([P, HALVES], F32, name="att_junk", tag="att_junk")
            nc.scalar.activation(out=att_junk[:], in_=att_ps[:], func=ACT.Copy, accum_out=att_sb[b][:])

        def t_out(b, h, on_vector):
            if h == 0:
                o_sb[b] = wrk.tile([P, HW], F32, name="o_sb", tag="o_sb", bufs=O_BUFS)
            dst = o_sb[b][:, h * N_TILE : (h + 1) * N_TILE]
            if on_vector:
                nc.vector.tensor_scalar_mul(out=dst, in0=t_ps[b, h][:], scalar1=att_sb[b][:, 0:1])
            else:
                nc.scalar.activation(out=dst, in_=t_ps[b, h][:], func=ACT.Copy, scale=att_sb[b][:, 0:1])

        def store(b):
            nc.sync.dma_start(out=ov[b], in_=o_sb[b][:])

        def load_w(w, ap):
            w_raw[w] = const.tile([P, K], BF16, name="w_raw_" + w)
            nc.sync.dma_start(out=w_raw[w][:], in_=ap)

        def w_transpose(w):
            w_ps[w] = psum.tile([P, PASSES * 2, P], F32, name="w_ps", tag=w, bufs=3 if w == "t" else 2)
            words = w_raw[w][:].bitcast(F32).rearrange("m (c p u) -> m c u p", c=PASSES, u=2)
            for c in range(PASSES):
                for u in range(2):
                    nc.tensor.transpose(w_ps[w][:, c * 2 + u, :], words[:, c, u, :], ident[:])

        def w_copy(w):
            cols = slice(w_base[w] * PACK, (w_base[w] + PASSES * P) * PACK)
            dst = w_grp[w][:, cols].bitcast(F32).rearrange("p (c m u) -> p c m u", c=PASSES, u=2)
            src = w_ps[w][:].rearrange("p (c u) m -> p c m u", c=PASSES)
            nc.scalar.copy(out=dst, in_=src)

        def w_quant(w):
            nc.vector.quantize_mx(
                out=w_codes[w][:].bitcast(FP8X4), scales=w_scales[w][:], in_=w_grp[w][:]
            )

        load(0)
        load_w("p", Wp)
        load_w("g", Wg)
        load(1)
        load_w("t", Wt)
        for n in range(2, CHUNKS):
            load(n)

        warm_in = const.tile([P, 1], F32, name="warm_in")
        warm_out = const.tile([P, 1], F32, name="warm_out")
        nc.vector.memset(warm_in[:], 0.0)
        nc.scalar.activation(out=warm_out[:], in_=warm_in[:], func=ACT.Copy)
        ident = const.tile([P, P], F32, name="ident")
        make_identity(nc, ident[:])
        grp8 = const.tile([P, P // GROUP], F32, name="grp8")
        nc.vector.reduce_sum(out=grp8[:], in_=ident[:].rearrange("p (j i) -> p j i", i=GROUP), axis=AX.X)
        blk = const.tile([P, P // GROUP, GROUP], F32, name="blk")
        nc.vector.tensor_copy(out=blk[:], in_=grp8[:].unsqueeze(2).to_broadcast([P, P // GROUP, GROUP]))
        blk2d = blk[:].rearrange("p j i -> p (j i)")
        ident_bf = const.tile([P, P], BF16, name="ident_bf")
        make_identity(nc, ident_bf[:])

        w_base = {"p": 0, "g": PASSES * P, "t": 0}
        pg_grp = const.tile([P, 2 * PASSES * P * PACK], BF16, name="pg_grp", align_bytes=64)
        pg_codes = const.tile([P, 2 * PASSES * P], U32, name="pg_codes", align_bytes=64)
        pg_scales = const.tile([P, 2 * PASSES * P], U8, name="pg_scales", align_bytes=64)
        t_grp = const.tile([P, PASSES * P * PACK], BF16, name="t_grp", align_bytes=64)
        t_codes = const.tile([P, PASSES * P], U32, name="t_codes", align_bytes=64)
        t_scales = const.tile([P, PASSES * P], U8, name="t_scales", align_bytes=64)
        for w in ("p", "g"):
            w_grp[w] = pg_grp
            w_codes[w] = pg_codes
            w_scales[w] = pg_scales
        w_grp["t"] = t_grp
        w_codes["t"] = t_codes
        w_scales["t"] = t_scales

        zeros = const.tile([P, N_TILE], BF16, name="zeros")
        nc.vector.memset(zeros[:], 0.0)
        warm_ps = psum.tile([P, N_TILE], F32, name="warm_ps", tag="t", bufs=3)

        def warm(count):
            for i in range(count):
                nc.tensor.matmul(warm_ps[:], lhsT=ident_bf[:], rhs=zeros[:], start=True, stop=True)

        warm(4)
        new_grouped(0)
        rg_pe(0)
        rg_v(0)
        rg_s(0)
        rg_out(0)
        w_transpose("p")
        w_transpose("g")
        warm(2)
        w_copy("p")
        w_copy("g")
        quant(0)
        w_quant("p")
        new_grouped(1)
        rg_pe(1)
        g_open(0, 0, 0)
        g_open(0, 1, 0)
        rg_v(1)
        rg_s(1)
        rg_out(1)
        w_transpose("t")
        w_copy("t")
        quant(1)
        w_quant("t")
        new_grouped(2)
        rg_pe(2)
        rg_v(2)
        rg_s(2)
        rg_out(2)
        mm_pg(0, 1)
        new_grouped(3)
        rg_s(3)
        p_copy(0, 0)
        p_copy(0, 1)
        rg_pe(3)
        rg_v(3)
        rg_out(3)

        att_tiles = {}

        def finish(b):
            t_out(b, 0, False)
            t_out(b, 1, False)
            store(b)

        for b in range(IMAGES - 2):
            if b > 0:
                mm_pg(b, 1)
                att_copy(b - 1, att_tiles[b - 1])
                p_copy(b, 0)
                p_copy(b, 1)
                finish(b - 1)
            quant(2 * b + 2)
            rg_pe(2 * b + 4)
            rg_pe(2 * b + 5)
            new_grouped(2 * b + 4)
            rg_v(2 * b + 4)
            rg_g(2 * b + 4)
            new_grouped(2 * b + 5)
            rg_s(2 * b + 4, EVEN_S)
            rg_s(2 * b + 5)
            pg_sum(b, 0)
            pg_sum(b, 1)
            mm_t(b, 0)
            mm_t(b, 1)
            att_tiles[b] = att_mm(b)
            g_open(b + 1, 0, 0)
            g_open(b + 1, 1, 0)
            rg_out(2 * b + 4)
            rg_out(2 * b + 5)
            quant(2 * b + 3)

        mm_pg(6, 1)
        att_copy(5, att_tiles[5])
        p_copy(6, 0)
        p_copy(6, 1)
        mm_t(6, 0)
        quant(14)
        quant(15, 0, N_TILE)
        pg_sum(6, 0)
        p_c0(7, 0)
        p_c1(7, 0)
        g_open(7, 0, 0)
        g_close(7, 0, 1)
        finish(5)
        p_copy(7, 0)
        quant(15, N_TILE, HW)
        pg_sum(6, 1)
        p_c0(7, 1)
        p_c1(7, 1)
        g_open(7, 1, 0)
        g_close(7, 1, 1)
        p_copy(7, 1)
        att_tiles[6] = att_mm(6)
        mm_t(6, 1)
        att_copy(6, att_tiles[6])
        pg_sum(7, 0)
        pg_sum(7, 1)
        t_out(6, 0, False)
        t_out(6, 1, True)
        store(6)
        mm_t(7, 0)
        att_ps = att_mm(7)
        mm_t(7, 1, "p")
        att_copy(7, att_ps)
        o_sb[7] = wrk.tile([P, HW], F32, name="o_sb", tag="o_sb", bufs=O_BUFS)
        for part in range(2):
            for h in range(HALVES):
                lo = part * (N_TILE // 2)
                hi = lo + N_TILE // 2
                dst = o_sb[7][:, h * N_TILE + lo : h * N_TILE + hi]
                if h == 1:
                    nc.vector.tensor_scalar_mul(out=dst, in0=t_ps[7, h][:, lo:hi], scalar1=att_sb[7][:, 0:1])
                else:
                    nc.scalar.activation(out=dst, in_=t_ps[7, h][:, lo:hi], func=ACT.Copy, scale=att_sb[7][:, 0:1])
            for h in range(HALVES):
                cols = slice(h * N_TILE + part * (N_TILE // 2), h * N_TILE + (part + 1) * (N_TILE // 2))
                nc.sync.dma_start(out=ov[7][:, cols], in_=o_sb[7][:, cols])
